import numpy as np
import ml_dtypes


def mxq(x, axis, fmt="e4m3"):
    dtype, down = {"e4m3": (ml_dtypes.float8_e4m3fn, 7), "e5m2": (ml_dtypes.float8_e5m2, 14)}[fmt]
    v = np.moveaxis(np.asarray(x, np.float32).astype(ml_dtypes.bfloat16).astype(np.float64), axis, -1)
    blocks = v.reshape(v.shape[:-1] + (-1, 32))
    amax = np.abs(blocks).max(-1, keepdims=True)
    byte = np.maximum(np.where(amax > 0, np.frexp(amax)[1] - 1 + 127, 0) - down, 1)
    scale = np.exp2(byte - 127.0)
    codes = (blocks / scale).astype(np.float32).astype(dtype).astype(np.float64)
    return np.moveaxis((codes * scale).reshape(v.shape), -1, axis)


WIDE = False


def mx_kscale(k):
    if not WIDE:
        return np.ones(k)
    levels = np.array([10, -10, 5, -5, 0])
    if k % 512:
        return np.exp2(np.random.permutation(np.resize(levels, k // 32))).repeat(32)
    a = np.empty((k // 512, 16))
    for p in range(k // 512):
        a[p, :8] = np.random.permutation(np.resize(levels, 8))
        for g in range(8):
            far = levels[np.abs(levels - a[p, g]) >= 10]
            a[p, g + 8] = far[np.random.randint(len(far))]
    return np.exp2(a.ravel()).repeat(32)


BF16 = ml_dtypes.bfloat16


def bf(x):
    return np.asarray(x, np.float32).astype(BF16)


def f64(x):
    return np.asarray(x).astype(np.float64)


B, S, D, M, R = 1024, 8, 512, 8, 512
LN_EPS = 1e-5


def sigmoid(v):
    return 1.0 / (1.0 + np.exp(-v))


def layer_norm(x):
    mu = np.mean(x, axis=-1, keepdims=True)
    var = np.var(x, axis=-1, keepdims=True)
    return (x - mu) / np.sqrt(var + LN_EPS)


def setup_inputs():
    s, t = mx_kscale(D), mx_kscale(R)
    return {"interface": bf(np.random.standard_normal((B, S, D)) * np.sqrt(S) * s),
            "memory": bf(0.5 + np.random.standard_normal((B, M, D))),
            "W_write_key": bf(np.random.standard_normal((R, D)) / np.sqrt(D) / s[None, :] * t[:, None]),
            "W_write_erase": bf(np.random.standard_normal((D, R)) * 1.5 / np.sqrt(R) / t[None, :]),
            "W_write_add": bf(np.random.standard_normal((D, R)) / np.sqrt(R) / t[None, :])}


def reference(interface, memory, W_write_key, W_write_erase, W_write_add):
    i_mean = np.mean(f64(interface), axis=1)
    i_proj = mxq(i_mean, 1, "e4m3") @ mxq(f64(W_write_key), 1, "e4m3").T
    pq = mxq(i_proj, 1, "e4m3")
    erase = sigmoid(pq @ mxq(f64(W_write_erase), 1, "e4m3").T)[:, None, :]
    add = (pq @ mxq(f64(W_write_add), 1, "e4m3").T)[:, None, :]
    return layer_norm(f64(memory) * (1.0 - erase) + add)

@@ -1,0 +1,396 @@
+from contextlib import ExitStack
+
+import concourse.mybir as mybir
+from concourse.masks import make_identity
+
+F32 = mybir.dt.float32
+BF16 = mybir.dt.bfloat16
+U32 = mybir.dt.uint32
+U8 = mybir.dt.uint8
+FP8X4 = mybir.dt.float8_e4m3fn_x4
+ALU = mybir.AluOpType
+ACT = mybir.ActivationFunctionType
+AX = mybir.AxisListType
+
+B, S, D, M, R = 1024, 8, 512, 8, 512
+LN_EPS = 1e-5
+P = 128
+NT = B // P
+KC = 4
+GB = P // S
+NG = P // GB
+FLOPS = 3 * 2 * B * D * R
+
+UNITS = [(i, 4 * h, 4 * h + 4) for i in range(NT - 1) for h in range(2)] + [
+    (NT - 1, 0, 4),
+    (NT - 1, 4, 6),
+    (NT - 1, 6, 8),
+]
+
+
+def tile_ultralightweightmemory_pa_t_kernel(
+    tc, interface, memory, W_write_key, W_write_erase, W_write_add, out
+):
+    nc = tc.nc
+    iview = interface.rearrange("b s d -> (b s) d").rearrange(
+        "(n g p) d -> n p g d", n=NT, g=NG, p=P
+    )
+    mview = memory.rearrange("(n p) m d -> n p m d", p=P)
+    oview = out.rearrange("(n p) m d -> n p m d", p=P)
+
+    with ExitStack() as ctx:
+        const = ctx.enter_context(tc.tile_pool(name="const", bufs=1))
+        ipool = ctx.enter_context(tc.tile_pool(name="ipool", bufs=5))
+        mpool = ctx.enter_context(tc.tile_pool(name="mpool", bufs=NT))
+        xpool = ctx.enter_context(tc.tile_pool(name="xpool", bufs=10))
+        wpool = ctx.enter_context(tc.tile_pool(name="wpool", bufs=2))
+        fpool = ctx.enter_context(tc.tile_pool(name="fpool", bufs=2))
+        spool = ctx.enter_context(tc.tile_pool(name="spool", bufs=6))
+        ps1 = ctx.enter_context(tc.psum_pool(name="ps1", bufs=1))
+        ps2 = ctx.enter_context(tc.psum_pool(name="ps2", bufs=2))
+        ctx.enter_context(tc.manual_schedule())
+
+        w_dram = [W_write_key, W_write_erase, W_write_add]
+        w_raw = []
+        for w in range(3):
+            wr = const.tile([P, KC, 512], BF16, name="w_raw%d" % w)
+            w_raw.append(wr)
+        i_tiles = []
+        m_tiles = []
+
+        def load_w(w):
+            nc.sync.dma_start(
+                out=w_raw[w][:],
+                in_=w_dram[w].rearrange("(p c) k -> p c k" if w == 0 else "(c p) k -> p c k", p=P),
+            )
+
+        def load_i(i):
+            it = ipool.tile([P, NG, D], BF16, name="it")
+            for h in range(2):
+                nc.sync.dma_start(
+                    out=it[:, 4 * h : 4 * h + 4, :], in_=iview[i][:, 4 * h : 4 * h + 4, :]
+                )
+            i_tiles.append(it)
+
+        def load_m(i):
+            mt = mpool.tile([P, M, D], BF16, name="mt")
+            nc.sync.dma_start(out=mt[:], in_=mview[i])
+            m_tiles.append(mt)
+
+        load_w(0)
+        load_i(0)
+        load_w(1)
+        load_w(2)
+        load_m(0)
+        for i in range(1, 5):
+            load_i(i)
+            load_m(i)
+
+        ident_bf = const.tile([P, P], BF16, name="ident_bf")
+        make_identity(nc, ident_bf[:])
+        ident_f = const.tile([P, P], F32, name="ident_f")
+        make_identity(nc, ident_f[:])
+        avg_f = const.tile([P, GB], F32, name="avg_f")
+        nc.vector.tensor_reduce(
+            out=avg_f[:],
+            in_=ident_f[:].rearrange("p (j s) -> p j s", s=S),
+            axis=AX.X,
+            op=ALU.add,
+        )
+        avg = const.tile([P, GB], BF16, name="avg")
+        nc.vector.tensor_scalar(
+            out=avg[:], in0=avg_f[:], scalar1=1.0 / S, scalar2=None, op0=ALU.mult
+        )
+        neghalf = const.tile([P, M], F32, name="neghalf")
+        nc.vector.memset(neghalf[:], -0.5)
+        junk = const.tile([P, D], BF16, name="junk")
+
+        w_codes = []
+        w_scales = []
+        for w in range(3):
+            wc = const.tile([P, 512], U32, name="w_codes%d" % w, align_bytes=64)
+            ws = const.tile([P, 512], U8, name="w_scales%d" % w, align_bytes=64)
+            w_codes.append(wc)
+            w_scales.append(ws)
+
+        def prep_weight(w):
+            grouped = wpool.tile([P, 512, KC], BF16, name="grouped", align_bytes=64)
+            for h in range(2):
+                wt = ps2.tile([P, 2, KC, P], BF16, name="wt", tag=("g_ps" if h == 0 else "a_ps"))
+                for c2 in range(2):
+                    for t in range(KC):
+                        nc.tensor.transpose(
+                            wt[:, c2, t, :],
+                            w_raw[w][:, 2 * h + c2, t : 512 : KC],
+                            ident_bf[:],
+                        )
+                dst = grouped[:, 256 * h : 256 * (h + 1), :].rearrange(
+                    "p (c r) t -> p c r t", c=2
+                )
+                src = wt[:].rearrange("p c t r -> p c r t")
+                if h == 0:
+                    nc.vector.tensor_copy(out=dst, in_=src)
+                else:
+                    nc.scalar.copy(out=dst, in_=src)
+            nc.vector.quantize_mx(
+                out=w_codes[w][:].bitcast(FP8X4),
+                scales=w_scales[w][:],
+                in_=grouped[:].rearrange("p r t -> p (r t)"),
+            )
+
+        fr = {}
+
+        def f1(j):
+            it = i_tiles[j]
+            mean_ps = ps1.tile([P, KC, P], F32, name="mean_ps")
+            for g in range(NG):
+                for t in range(KC):
+                    nc.tensor.matmul(
+                        out=mean_ps[:, t, GB * g : GB * (g + 1)],
+                        lhsT=it[:, g, t : D : KC],
+                        rhs=avg[:],
+                        start=True,
+                        stop=True,
+                    )
+            fr[j] = {"mean_ps": mean_ps}
+
+        def f2(j):
+            im_g = fpool.tile([P, P, KC], BF16, name="im_g", align_bytes=64)
+            nc.scalar.copy(out=im_g[:], in_=fr[j]["mean_ps"][:].rearrange("p t b -> p b t"))
+            fr[j]["im_g"] = im_g
+
+        def quant(j, src, dst):
+            codes = fpool.tile([P, P], U32, name=dst + "_c", align_bytes=64)
+            scales = fpool.tile([P, P], U8, name=dst + "_s", align_bytes=64)
+            nc.vector.quantize_mx(
+                out=codes[:].bitcast(FP8X4),
+                scales=scales[:],
+                in_=fr[j][src][:].rearrange("p b t -> p (b t)"),
+            )
+            fr[j][dst] = (codes, scales)
+
+        def mx_t(j, w, src, dst):
+            codes, scales = fr[j][src]
+            acc = ps1.tile([P, KC, P], F32, name=dst)
+            for c in range(KC):
+                nc.tensor.matmul_mx(
+                    out=acc[:, c, :],
+                    lhsT=w_codes[w][:, c * P : (c + 1) * P].bitcast(FP8X4),
+                    lhsT_scale=w_scales[w][:, c * P : (c + 1) * P],
+                    rhs=codes[:].bitcast(FP8X4),
+                    rhs_scale=scales[:],
+                    start=True,
+                    stop=True,
+                )
+            fr[j][dst] = acc
+
+        def f3(j):
+            quant(j, "im_g", "im")
+
+        def f4(j):
+            mx_t(j, 0, "im", "s1_ps")
+
+        def f5(j):
+            pj_g = fpool.tile([P, P, KC], BF16, name="pj_g", align_bytes=64)
+            nc.scalar.copy(out=pj_g[:], in_=fr[j]["s1_ps"][:].rearrange("p c b -> p b c"))
+            fr[j]["pj_g"] = pj_g
+
+        def f6(j):
+            quant(j, "pj_g", "pq")
+
+        def f7(j):
+            mx_t(j, 1, "pq", "et_ps")
+            codes, scales = fr[j]["pq"]
+            a_ps = ps2.tile([P, D], F32, name="a_ps")
+            nc.tensor.matmul_mx(
+                out=a_ps[:],
+                lhsT=codes[:].bitcast(FP8X4),
+                lhsT_scale=scales[:],
+                rhs=w_codes[2][:].bitcast(FP8X4),
+                rhs_scale=w_scales[2][:],
+                start=True,
+                stop=True,
+            )
+            fr[j]["a_ps"] = a_ps
+
+        def f8(j):
+            g_t = fpool.tile([P, KC, P], F32, name="g_t")
+            nc.scalar.activation(out=g_t[:], in_=fr[j]["et_ps"][:], func=ACT.Sigmoid, scale=-1.0)
+            fr[j]["g_t"] = g_t
+
+        def f9(j):
+            g_ps = ps2.tile([P, D], F32, name="g_ps")
+            for c in range(KC):
+                nc.tensor.transpose(
+                    g_ps[:, c * P : (c + 1) * P], fr[j]["g_t"][:, c, :], ident_f[:]
+                )
+            fr[j]["g_ps"] = g_ps
+
+        NU = len(UNITS)
+        st = {}
+
+        def p1(u):
+            i, m0, m1 = UNITS[u]
+            n = m1 - m0
+            x = xpool.tile([P, 4, D], F32, name="x")
+            nc.vector.tensor_tensor(
+                out=x[:, 0:n, :],
+                in0=m_tiles[i][:, m0:m1, :],
+                in1=fr[i]["g_ps"][:].unsqueeze(1).to_broadcast([P, n, D]),
+                op=ALU.mult,
+            )
+            st[u] = {"x": x, "n": n}
+
+        def p2(u):
+            i, m0, m1 = UNITS[u]
+            x = st[u]["x"]
+            sums = spool.tile([P, 4], F32, name="sums")
+            for m in range(st[u]["n"]):
+                nc.vector.scalar_tensor_tensor(
+                    out=x[:, m, :],
+                    in0=x[:, m, :],
+                    scalar=1.0,
+                    in1=fr[i]["a_ps"][:],
+                    op0=ALU.mult,
+                    op1=ALU.add,
+                    accum_out=sums[:, m : m + 1],
+                )
+            st[u]["sums"] = sums
+
+        def nmean(u):
+            n = st[u]["n"]
+            nm = spool.tile([P, 4], F32, name="nm")
+            nc.scalar.mul(out=nm[:, 0:n], in_=st[u]["sums"][:, 0:n], mul=-1.0 / D)
+            st[u]["nm"] = nm
+            ssq = spool.tile([P, 4], F32, name="ssq")
+            st[u]["ssq"] = ssq
+
+        def p3(u, ms):
+            for m in ms:
+                nc.scalar.activation(
+                    out=junk[:],
+                    in_=st[u]["x"][:, m, :],
+                    func=ACT.Square,
+                    bias=st[u]["nm"][:, m : m + 1],
+                    scale=1.0,
+                    accum_out=st[u]["ssq"][:, m : m + 1],
+                )
+
+        def chain(u):
+            n = st[u]["n"]
+            ve = spool.tile([P, 4], F32, name="ve")
+            nc.gpsimd.tensor_scalar(
+                out=ve[:, 0:n],
+                in0=st[u]["ssq"][:, 0:n],
+                scalar1=1.0 / D,
+                scalar2=LN_EPS,
+                op0=ALU.mult,
+                op1=ALU.add,
+            )
+            rstd = spool.tile([P, 4], F32, name="rstd")
+            nc.gpsimd.tensor_tensor(
+                out=rstd[:, 0:n], in0=ve[:, 0:n], in1=neghalf[:, 0:n], op=ALU.pow
+            )
+            nb = spool.tile([P, 4], F32, name="nb")
+            nc.gpsimd.tensor_tensor(
+                out=nb[:, 0:n], in0=st[u]["nm"][:, 0:n], in1=rstd[:, 0:n], op=ALU.mult
+            )
+            st[u]["rstd"] = rstd
+            st[u]["nb"] = nb
+
+        def p4s(u):
+            x = st[u]["x"]
+            for m in range(st[u]["n"] // 2):
+                nc.scalar.activation(
+                    out=x[:, m, :],
+                    in_=x[:, m, :],
+                    func=ACT.Identity,
+                    bias=st[u]["nb"][:, m : m + 1],
+                    scale=st[u]["rstd"][:, m : m + 1],
+                )
+
+        def p4g(u):
+            x = st[u]["x"]
+            for m in range(st[u]["n"] // 2, st[u]["n"]):
+                nc.gpsimd.tensor_scalar(
+                    out=x[:, m, :],
+                    in0=x[:, m, :],
+                    scalar1=st[u]["nm"][:, m : m + 1],
+                    scalar2=st[u]["rstd"][:, m : m + 1],
+                    op0=ALU.add,
+                    op1=ALU.mult,
+                )
+
+        def store(u):
+            i, m0, m1 = UNITS[u]
+            nc.sync.dma_start(out=oview[i][:, m0:m1, :], in_=st[u]["x"][:, 0 : m1 - m0, :])
+
+        prep_weight(0)
+        f1(0)
+        f2(0)
+        f3(0)
+        prep_weight(1)
+        f4(0)
+        f5(0)
+        f6(0)
+        prep_weight(2)
+        f7(0)
+        f8(0)
+        f9(0)
+        f1(1)
+        f2(1)
+
+        late_loads = {2: ("i", 5), 3: ("i", 6), 4: ("i", 7), 5: ("m", 5), 6: ("m", 6), 7: ("m", 7)}
+
+        for u in range(NU + 2):
+            even = u % 2 == 0
+            j = (u + 2) // 2 if even else (u + 3) // 2
+            fj = 2 <= j < NT
+            if fj and even:
+                f4(j)
+            if fj and not even:
+                f1(j)
+            if u < NU:
+                p1(u)
+            if u == 0:
+                f3(1)
+                f4(1)
+                f5(1)
+            if 1 <= u <= NU:
+                nmean(u - 1)
+                p3(u - 1, [0])
+            if fj and even:
+                f5(j)
+                f6(j)
+            if 1 <= u <= NU:
+                p3(u - 1, range(1, st[u - 1]["n"]))
+            if fj and even:
+                f7(j)
+            if u < NU:
+                p2(u)
+            if u == 0:
+                f6(1)
+                f7(1)
+                f8(1)
+                f9(1)
+            if u >= 2:
+                p4g(u - 2)
+            if 1 <= u <= NU:
+                chain(u - 1)
+            if fj and not even:
+                f2(j)
+            if u >= 2:
+                p4s(u - 2)
+            if fj and even:
+                f8(j)
+                f9(j)
+            if fj and not even:
+                f3(j)
+            if u >= 2:
+                store(u - 2)
+            if u in late_loads:
+                kind, idx = late_loads[u]
+                if kind == "i":
+                    load_i(idx)
+                else:
+                    load_m(idx)

@@ -21,11 +21,8 @@ GB = P // S
 NG = P // GB
 FLOPS = 3 * 2 * B * D * R
 
-UNITS = [(i, 4 * h, 4 * h + 4) for i in range(NT - 1) for h in range(2)] + [
-    (NT - 1, 0, 4),
-    (NT - 1, 4, 6),
-    (NT - 1, 6, 8),
-]
+ADD_G = (3, 7)
+NORM_S = (0, 4)
 
 
 def tile_ultralightweightmemory_pa_t_kernel(
@@ -40,12 +37,12 @@ def tile_ultralightweightmemory_pa_t_kernel(
 
     with ExitStack() as ctx:
         const = ctx.enter_context(tc.tile_pool(name="const", bufs=1))
-        ipool = ctx.enter_context(tc.tile_pool(name="ipool", bufs=5))
+        ipool = ctx.enter_context(tc.tile_pool(name="ipool", bufs=6))
         mpool = ctx.enter_context(tc.tile_pool(name="mpool", bufs=NT))
-        xpool = ctx.enter_context(tc.tile_pool(name="xpool", bufs=10))
+        xpool = ctx.enter_context(tc.tile_pool(name="xpool", bufs=5))
         wpool = ctx.enter_context(tc.tile_pool(name="wpool", bufs=2))
         fpool = ctx.enter_context(tc.tile_pool(name="fpool", bufs=2))
-        spool = ctx.enter_context(tc.tile_pool(name="spool", bufs=6))
+        spool = ctx.enter_context(tc.tile_pool(name="spool", bufs=4))
         ps1 = ctx.enter_context(tc.psum_pool(name="ps1", bufs=1))
         ps2 = ctx.enter_context(tc.psum_pool(name="ps2", bufs=2))
         ctx.enter_context(tc.manual_schedule())
@@ -81,13 +78,19 @@ def tile_ultralightweightmemory_pa_t_kernel(
         load_i(0)
         load_w(1)
         load_w(2)
+        load_i(1)
         load_m(0)
-        for i in range(1, 5):
+        load_i(2)
+        load_m(1)
+        for i in range(3, 6):
             load_i(i)
-            load_m(i)
+            load_m(i - 1)
 
-        ident_bf = const.tile([P, P], BF16, name="ident_bf")
-        make_identity(nc, ident_bf[:])
+        junk = const.tile([P, 2, D], BF16, name="junk")
+        junk_v = const.tile([P, D], BF16, name="junk_v")
+        neghalf = const.tile([P, M], F32, name="neghalf")
+        nc.vector.memset(neghalf[:], -0.5)
+        nc.scalar.activation(out=junk[:, 0, 0:1], in_=neghalf[:, 0:1], func=ACT.Sigmoid)
         ident_f = const.tile([P, P], F32, name="ident_f")
         make_identity(nc, ident_f[:])
         avg_f = const.tile([P, GB], F32, name="avg_f")
@@ -101,9 +104,6 @@ def tile_ultralightweightmemory_pa_t_kernel(
         nc.vector.tensor_scalar(
             out=avg[:], in0=avg_f[:], scalar1=1.0 / S, scalar2=None, op0=ALU.mult
         )
-        neghalf = const.tile([P, M], F32, name="neghalf")
-        nc.vector.memset(neghalf[:], -0.5)
-        junk = const.tile([P, D], BF16, name="junk")
 
         w_codes = []
         w_scales = []
@@ -115,19 +115,22 @@ def tile_ultralightweightmemory_pa_t_kernel(
 
         def prep_weight(w):
             grouped = wpool.tile([P, 512, KC], BF16, name="grouped", align_bytes=64)
+            words = w_raw[w][:].rearrange("p c k -> p (c k)").bitcast(F32)
             for h in range(2):
-                wt = ps2.tile([P, 2, KC, P], BF16, name="wt", tag=("g_ps" if h == 0 else "a_ps"))
+                wt = ps2.tile([P, 2, 2, P], F32, name="wt", tag=("g_ps" if h == 0 else "a_ps"))
                 for c2 in range(2):
-                    for t in range(KC):
+                    for u in range(2):
+                        base = (2 * h + c2) * 256
                         nc.tensor.transpose(
-                            wt[:, c2, t, :],
-                            w_raw[w][:, 2 * h + c2, t : 512 : KC],
-                            ident_bf[:],
+                            wt[:, c2, u, :], words[:, base + u : base + 256 : 2], ident_f[:]
                         )
-                dst = grouped[:, 256 * h : 256 * (h + 1), :].rearrange(
-                    "p (c r) t -> p c r t", c=2
+                dst = (
+                    grouped[:]
+                    .rearrange("p r t -> p (r t)")
+                    .bitcast(F32)[:, 512 * h : 512 * (h + 1)]
+                    .rearrange("p (c r u) -> p c r u", c=2, u=2)
                 )
-                src = wt[:].rearrange("p c t r -> p c r t")
+                src = wt[:].rearrange("p c u r -> p c r u")
                 if h == 0:
                     nc.vector.tensor_copy(out=dst, in_=src)
                 else:
@@ -140,10 +143,13 @@ def tile_ultralightweightmemory_pa_t_kernel(
 
         fr = {}
 
-        def f1(j):
+        def f1(j, g0, g1):
             it = i_tiles[j]
-            mean_ps = ps1.tile([P, KC, P], F32, name="mean_ps")
-            for g in range(NG):
+            if g0 == 0:
+                mean_ps = ps1.tile([P, KC, P], F32, name="mean_ps")
+                fr[j] = {"mean_ps": mean_ps}
+            mean_ps = fr[j]["mean_ps"]
+            for g in range(g0, g1):
                 for t in range(KC):
                     nc.tensor.matmul(
                         out=mean_ps[:, t, GB * g : GB * (g + 1)],
@@ -152,7 +158,6 @@ def tile_ultralightweightmemory_pa_t_kernel(
                         start=True,
                         stop=True,
                     )
-            fr[j] = {"mean_ps": mean_ps}
 
         def f2(j):
             im_g = fpool.tile([P, P, KC], BF16, name="im_g", align_bytes=64)
@@ -200,6 +205,8 @@ def tile_ultralightweightmemory_pa_t_kernel(
 
         def f7(j):
             mx_t(j, 1, "pq", "et_ps")
+
+        def f7a(j):
             codes, scales = fr[j]["pq"]
             a_ps = ps2.tile([P, D], F32, name="a_ps")
             nc.tensor.matmul_mx(
@@ -218,6 +225,17 @@ def tile_ultralightweightmemory_pa_t_kernel(
             nc.scalar.activation(out=g_t[:], in_=fr[j]["et_ps"][:], func=ACT.Sigmoid, scale=-1.0)
             fr[j]["g_t"] = g_t
 
+        def f8a(j):
+            a_sb = fpool.tile([P, D], F32, name="a_sb")
+            a_sum = spool.tile([P, 1], F32, name="a_sum")
+            nc.scalar.activation(
+                out=a_sb[:], in_=fr[j]["a_ps"][:], func=ACT.Identity, accum_out=a_sum[:]
+            )
+            na = spool.tile([P, 1], F32, name="na")
+            nc.scalar.mul(out=na[:], in_=a_sum[:], mul=-1.0 / D)
+            fr[j]["a_sb"] = a_sb
+            fr[j]["na"] = na
+
         def f9(j):
             g_ps = ps2.tile([P, D], F32, name="g_ps")
             for c in range(KC):
@@ -226,107 +244,155 @@ def tile_ultralightweightmemory_pa_t_kernel(
                 )
             fr[j]["g_ps"] = g_ps
 
-        NU = len(UNITS)
-        st = {}
+        st = []
+        for i in range(NT):
+            st.append({})
 
-        def p1(u):
-            i, m0, m1 = UNITS[u]
-            n = m1 - m0
-            x = xpool.tile([P, 4, D], F32, name="x")
-            nc.vector.tensor_tensor(
-                out=x[:, 0:n, :],
-                in0=m_tiles[i][:, m0:m1, :],
-                in1=fr[i]["g_ps"][:].unsqueeze(1).to_broadcast([P, n, D]),
-                op=ALU.mult,
-            )
-            st[u] = {"x": x, "n": n}
-
-        def p2(u):
-            i, m0, m1 = UNITS[u]
-            x = st[u]["x"]
-            sums = spool.tile([P, 4], F32, name="sums")
-            for m in range(st[u]["n"]):
+        def p1(i, m0, m1):
+            if m0 == 0:
+                x = xpool.tile([P, M, D], F32, name="x")
+                sums = spool.tile([P, M], F32, name="sums")
+                ssq = spool.tile([P, M], F32, name="ssq")
+                st[i] = {"x": x, "sums": sums, "ssq": ssq}
+            for m in range(m0, m1):
                 nc.vector.scalar_tensor_tensor(
-                    out=x[:, m, :],
-                    in0=x[:, m, :],
+                    out=st[i]["x"][:, m, :],
+                    in0=m_tiles[i][:, m, :],
                     scalar=1.0,
-                    in1=fr[i]["a_ps"][:],
+                    in1=fr[i]["g_ps"][:],
                     op0=ALU.mult,
-                    op1=ALU.add,
-                    accum_out=sums[:, m : m + 1],
+                    op1=ALU.mult,
+                    accum_out=st[i]["sums"][:, m : m + 1],
                 )
-            st[u]["sums"] = sums
 
-        def nmean(u):
-            n = st[u]["n"]
-            nm = spool.tile([P, 4], F32, name="nm")
-            nc.scalar.mul(out=nm[:, 0:n], in_=st[u]["sums"][:, 0:n], mul=-1.0 / D)
-            st[u]["nm"] = nm
-            ssq = spool.tile([P, 4], F32, name="ssq")
-            st[u]["ssq"] = ssq
+        def p2v(i, m0, m1):
+            x = st[i]["x"]
+            nc.vector.tensor_tensor(
+                out=x[:, m0:m1, :],
+                in0=x[:, m0:m1, :],
+                in1=fr[i]["a_ps"][:].unsqueeze(1).to_broadcast([P, m1 - m0, D]),
+                op=ALU.add,
+            )
 
-        def p3(u, ms):
+        def p2g(i, m):
+            x = st[i]["x"]
+            nc.gpsimd.tensor_tensor(
+                out=x[:, m, :], in0=x[:, m, :], in1=fr[i]["a_sb"][:], op=ALU.add
+            )
+
+        def nmean(i, m0, m1):
+            if m0 == 0:
+                nm = spool.tile([P, M], F32, name="nm")
+                st[i]["nm"] = nm
+            nc.scalar.activation(
+                out=st[i]["nm"][:, m0:m1],
+                in_=st[i]["sums"][:, m0:m1],
+                func=ACT.Identity,
+                scale=-1.0 / D,
+                bias=fr[i]["na"][:],
+            )
+
+        def p3(i, ms):
             for m in ms:
                 nc.scalar.activation(
-                    out=junk[:],
-                    in_=st[u]["x"][:, m, :],
+                    out=junk[:, m % 2, :],
+                    in_=st[i]["x"][:, m, :],
                     func=ACT.Square,
-                    bias=st[u]["nm"][:, m : m + 1],
+                    bias=st[i]["nm"][:, m : m + 1],
                     scale=1.0,
-                    accum_out=st[u]["ssq"][:, m : m + 1],
+                    accum_out=st[i]["ssq"][:, m : m + 1],
                 )
 
-        def chain(u):
-            n = st[u]["n"]
-            ve = spool.tile([P, 4], F32, name="ve")
+        def chain(i, m0, m1):
+            if m0 == 0:
+                ve = spool.tile([P, M], F32, name="ve")
+                rstd = spool.tile([P, M], F32, name="rstd")
+                nb = spool.tile([P, M], F32, name="nb")
+                st[i]["ve"] = ve
+                st[i]["rstd"] = rstd
+                st[i]["nb"] = nb
+            ve = st[i]["ve"]
+            rstd = st[i]["rstd"]
             nc.gpsimd.tensor_scalar(
-                out=ve[:, 0:n],
-                in0=st[u]["ssq"][:, 0:n],
+                out=ve[:, m0:m1],
+                in0=st[i]["ssq"][:, m0:m1],
                 scalar1=1.0 / D,
                 scalar2=LN_EPS,
                 op0=ALU.mult,
                 op1=ALU.add,
             )
-            rstd = spool.tile([P, 4], F32, name="rstd")
             nc.gpsimd.tensor_tensor(
-                out=rstd[:, 0:n], in0=ve[:, 0:n], in1=neghalf[:, 0:n], op=ALU.pow
+                out=rstd[:, m0:m1], in0=ve[:, m0:m1], in1=neghalf[:, m0:m1], op=ALU.pow
             )
-            nb = spool.tile([P, 4], F32, name="nb")
             nc.gpsimd.tensor_tensor(
-                out=nb[:, 0:n], in0=st[u]["nm"][:, 0:n], in1=rstd[:, 0:n], op=ALU.mult
+                out=st[i]["nb"][:, m0:m1],
+                in0=st[i]["nm"][:, m0:m1],
+                in1=rstd[:, m0:m1],
+                op=ALU.mult,
             )
-            st[u]["rstd"] = rstd
-            st[u]["nb"] = nb
 
-        def p4s(u):
-            x = st[u]["x"]
-            for m in range(st[u]["n"] // 2):
+        def root(i, m0, m1):
+            std = spool.tile([P, M], F32, name="std")
+            nc.scalar.activation(
+                out=std[:, m0:m1],
+                in_=st[i]["ssq"][:, m0:m1],
+                func=ACT.Sqrt,
+                scale=1.0 / D,
+                bias=LN_EPS,
+            )
+            if m0 == 0:
+                rstd = spool.tile([P, M], F32, name="rstd")
+                st[i]["rstd"] = rstd
+                nb = spool.tile([P, M], F32, name="nb")
+                st[i]["nb"] = nb
+            nc.vector.reciprocal(out=st[i]["rstd"][:, m0:m1], in_=std[:, m0:m1])
+            nc.vector.tensor_tensor(
+                out=st[i]["nb"][:, m0:m1],
+                in0=st[i]["nm"][:, m0:m1],
+                in1=st[i]["rstd"][:, m0:m1],
+                op=ALU.mult,
+            )
+
+        def p3v(i, ms):
+            for m in ms:
+                nc.vector.scalar_tensor_tensor(
+                    out=junk_v[:],
+                    in0=st[i]["x"][:, m, :],
+                    scalar=st[i]["nm"][:, m : m + 1],
+                    in1=st[i]["x"][:, m, :],
+                    op0=ALU.add,
+                    op1=ALU.mult,
+                    accum_out=st[i]["ssq"][:, m : m + 1],
+                )
+
+        def p4s(i, ms):
+            x = st[i]["x"]
+            for m in ms:
                 nc.scalar.activation(
                     out=x[:, m, :],
                     in_=x[:, m, :],
                     func=ACT.Identity,
-                    bias=st[u]["nb"][:, m : m + 1],
-                    scale=st[u]["rstd"][:, m : m + 1],
+                    bias=st[i]["nb"][:, m : m + 1],
+                    scale=st[i]["rstd"][:, m : m + 1],
                 )
 
-        def p4g(u):
-            x = st[u]["x"]
-            for m in range(st[u]["n"] // 2, st[u]["n"]):
-                nc.gpsimd.tensor_scalar(
+        def p4(engine, i, ms):
+            x = st[i]["x"]
+            for m in ms:
+                engine.tensor_scalar(
                     out=x[:, m, :],
                     in0=x[:, m, :],
-                    scalar1=st[u]["nm"][:, m : m + 1],
-                    scalar2=st[u]["rstd"][:, m : m + 1],
+                    scalar1=st[i]["nm"][:, m : m + 1],
+                    scalar2=st[i]["rstd"][:, m : m + 1],
                     op0=ALU.add,
                     op1=ALU.mult,
                 )
 
-        def store(u):
-            i, m0, m1 = UNITS[u]
-            nc.sync.dma_start(out=oview[i][:, m0:m1, :], in_=st[u]["x"][:, 0 : m1 - m0, :])
+        def store(i, m0, m1):
+            nc.sync.dma_start(out=oview[i][:, m0:m1, :], in_=st[i]["x"][:, m0:m1, :])
 
         prep_weight(0)
-        f1(0)
+        f1(0, 0, 8)
         f2(0)
         f3(0)
         prep_weight(1)
@@ -335,62 +401,115 @@ def tile_ultralightweightmemory_pa_t_kernel(
         f6(0)
         prep_weight(2)
         f7(0)
+        f1(1, 0, 2)
         f8(0)
         f9(0)
-        f1(1)
+        f7a(0)
+        f1(1, 2, 8)
+        f8a(0)
+        load_m(5)
+        load_i(6)
+        load_m(6)
+        load_i(7)
+        load_m(7)
+
+        p1(0, 0, 7)
         f2(1)
+        f3(1)
+        f4(1)
+        f1(2, 0, 4)
+        f5(1)
+        p1(0, 7, 8)
+        p2v(0, 0, 3)
+        f6(1)
+        f7(1)
+        f8(1)
+        f9(1)
+        f7a(1)
+        f1(2, 4, 8)
+        p2g(0, 3)
+        nmean(0, 0, 8)
+        p3(0, [0, 1])
+        p2v(0, 4, 7)
+        f8a(1)
 
-        late_loads = {2: ("i", 5), 3: ("i", 6), 4: ("i", 7), 5: ("m", 5), 6: ("m", 6), 7: ("m", 7)}
+        LAST = NT - 1
+        for i in range(1, NT - 1):
+            p1(i, 0, 4)
+            p3(i - 1, [0] if i > 1 else [])
+            f2(i + 1)
+            f3(i + 1)
+            f4(i + 1)
+            p3(i - 1, [1, 2, 3] if i > 1 else [2, 3])
+            if i + 2 < NT:
+                f1(i + 2, 0, 4)
+            if i >= 2:
+                p4(nc.gpsimd, i - 2, [5, 6, 7])
+                p4s(i - 2, [4])
+                store(i - 2, 4, 8)
+            p2g(i - 1, 7)
+            chain(i - 1, 0, 4)
+            f5(i + 1)
+            if i == 1:
+                p1(i, 4, 8)
+            else:
+                p2v(i - 1, 4, 7)
+            p3(i - 1, [4, 5])
+            f6(i + 1)
+            f7(i + 1)
+            f8(i + 1)
+            f9(i + 1)
+            f7a(i + 1)
+            p4(nc.gpsimd, i - 1, [1, 2, 3])
+            if i + 2 < NT:
+                f1(i + 2, 4, 8)
+            p2g(i, 3)
+            p3(i - 1, [6])
+            p4s(i - 1, [0])
+            p3(i - 1, [7])
+            chain(i - 1, 4, 8)
+            store(i - 1, 0, 4)
+            if i >= 2:
+                p1(i, 4, 8)
+            p2v(i, 0, 3)
+            nmean(i, 0, 8)
+            f8a(i + 1)
 
-        for u in range(NU + 2):
-            even = u % 2 == 0
-            j = (u + 2) // 2 if even else (u + 3) // 2
-            fj = 2 <= j < NT
-            if fj and even:
-                f4(j)
-            if fj and not even:
-                f1(j)
-            if u < NU:
-                p1(u)
-            if u == 0:
-                f3(1)
-                f4(1)
-                f5(1)
-            if 1 <= u <= NU:
-                nmean(u - 1)
-                p3(u - 1, [0])
-            if fj and even:
-                f5(j)
-                f6(j)
-            if 1 <= u <= NU:
-                p3(u - 1, range(1, st[u - 1]["n"]))
-            if fj and even:
-                f7(j)
-            if u < NU:
-                p2(u)
-            if u == 0:
-                f6(1)
-                f7(1)
-                f8(1)
-                f9(1)
-            if u >= 2:
-                p4g(u - 2)
-            if 1 <= u <= NU:
-                chain(u - 1)
-            if fj and not even:
-                f2(j)
-            if u >= 2:
-                p4s(u - 2)
-            if fj and even:
-                f8(j)
-                f9(j)
-            if fj and not even:
-                f3(j)
-            if u >= 2:
-                store(u - 2)
-            if u in late_loads:
-                kind, idx = late_loads[u]
-                if kind == "i":
-                    load_i(idx)
-                else:
-                    load_m(idx)
+        p1(LAST, 0, 4)
+        p3(LAST - 1, [0, 1, 2, 3])
+        p4(nc.gpsimd, LAST - 2, [5, 6, 7])
+        p2g(LAST - 1, 7)
+        nc.scalar.activation(out=junk[:, 0, 0:1], in_=neghalf[:, 0:1], func=ACT.Square)
+        nc.scalar.activation(out=junk[:, 1, 0:1], in_=junk[:, 0, 0:1], func=ACT.Sqrt)
+        p2v(LAST - 1, 4, 7)
+        root(LAST - 1, 0, 4)
+        p4(nc.gpsimd, LAST - 1, [1, 2, 3])
+        p4s(LAST - 2, [4])
+        store(LAST - 2, 4, 8)
+        nmean(LAST, 0, 4)
+        p2v(LAST, 0, 4)
+        p3(LAST - 1, [4, 5, 6, 7])
+        p4s(LAST - 1, [0])
+        store(LAST - 1, 0, 4)
+        p1(LAST, 4, 7)
+        root(LAST - 1, 4, 8)
+        p4(nc.gpsimd, LAST - 1, [4, 5, 6, 7])
+        store(LAST - 1, 4, 8)
+        p1(LAST, 7, 8)
+        p3(LAST, [0, 1, 2])
+        nmean(LAST, 4, 8)
+        p2v(LAST, 4, 6)
+        p3(LAST, [3])
+        p2v(LAST, 6, 8)
+        root(LAST, 0, 4)
+        p3(LAST, [4, 5])
+        p3v(LAST, [6])
+        p4(nc.vector, LAST, [0, 1, 2, 3])
+        store(LAST, 0, 4)
+        p3(LAST, [7])
+        root(LAST, 4, 8)
+        p4(nc.vector, LAST, [4, 5])
+        store(LAST, 4, 6)
+        p4(nc.vector, LAST, [6])
+        p4s(LAST, [7])
+        store(LAST, 6, 8)

@@ -21,9 +21,6 @@ GB = P // S
 NG = P // GB
 FLOPS = 3 * 2 * B * D * R
 
-ADD_G = (3, 7)
-NORM_S = (0, 4)
-
 
 def tile_ultralightweightmemory_pa_t_kernel(
     tc, interface, memory, W_write_key, W_write_erase, W_write_add, out
@@ -225,17 +222,6 @@ def tile_ultralightweightmemory_pa_t_kernel(
             nc.scalar.activation(out=g_t[:], in_=fr[j]["et_ps"][:], func=ACT.Sigmoid, scale=-1.0)
             fr[j]["g_t"] = g_t
 
-        def f8a(j):
-            a_sb = fpool.tile([P, D], F32, name="a_sb")
-            a_sum = spool.tile([P, 1], F32, name="a_sum")
-            nc.scalar.activation(
-                out=a_sb[:], in_=fr[j]["a_ps"][:], func=ACT.Identity, accum_out=a_sum[:]
-            )
-            na = spool.tile([P, 1], F32, name="na")
-            nc.scalar.mul(out=na[:], in_=a_sum[:], mul=-1.0 / D)
-            fr[j]["a_sb"] = a_sb
-            fr[j]["na"] = na
-
         def f9(j):
             g_ps = ps2.tile([P, D], F32, name="g_ps")
             for c in range(KC):
@@ -252,44 +238,32 @@ def tile_ultralightweightmemory_pa_t_kernel(
             if m0 == 0:
                 x = xpool.tile([P, M, D], F32, name="x")
                 sums = spool.tile([P, M], F32, name="sums")
+                nm = spool.tile([P, M], F32, name="nm")
                 ssq = spool.tile([P, M], F32, name="ssq")
-                st[i] = {"x": x, "sums": sums, "ssq": ssq}
-            for m in range(m0, m1):
+                st[i] = {"x": x, "sums": sums, "nm": nm, "ssq": ssq}
+            nc.vector.tensor_tensor(
+                out=st[i]["x"][:, m0:m1, :],
+                in0=m_tiles[i][:, m0:m1, :],
+                in1=fr[i]["g_ps"][:].unsqueeze(1).to_broadcast([P, m1 - m0, D]),
+                op=ALU.mult,
+            )
+
+        def p2(i, ms):
+            x = st[i]["x"]
+            for m in ms:
                 nc.vector.scalar_tensor_tensor(
-                    out=st[i]["x"][:, m, :],
-                    in0=m_tiles[i][:, m, :],
+                    out=x[:, m, :],
+                    in0=x[:, m, :],
                     scalar=1.0,
-                    in1=fr[i]["g_ps"][:],
+                    in1=fr[i]["a_ps"][:],
                     op0=ALU.mult,
-                    op1=ALU.mult,
+                    op1=ALU.add,
                     accum_out=st[i]["sums"][:, m : m + 1],
                 )
 
-        def p2v(i, m0, m1):
-            x = st[i]["x"]
-            nc.vector.tensor_tensor(
-                out=x[:, m0:m1, :],
-                in0=x[:, m0:m1, :],
-                in1=fr[i]["a_ps"][:].unsqueeze(1).to_broadcast([P, m1 - m0, D]),
-                op=ALU.add,
-            )
-
-        def p2g(i, m):
-            x = st[i]["x"]
-            nc.gpsimd.tensor_tensor(
-                out=x[:, m, :], in0=x[:, m, :], in1=fr[i]["a_sb"][:], op=ALU.add
-            )
-
         def nmean(i, m0, m1):
-            if m0 == 0:
-                nm = spool.tile([P, M], F32, name="nm")
-                st[i]["nm"] = nm
-            nc.scalar.activation(
-                out=st[i]["nm"][:, m0:m1],
-                in_=st[i]["sums"][:, m0:m1],
-                func=ACT.Identity,
-                scale=-1.0 / D,
-                bias=fr[i]["na"][:],
+            nc.scalar.mul(
+                out=st[i]["nm"][:, m0:m1], in_=st[i]["sums"][:, m0:m1], mul=-1.0 / D
             )
 
         def p3(i, ms):
@@ -406,54 +380,53 @@ def tile_ultralightweightmemory_pa_t_kernel(
         f9(0)
         f7a(0)
         f1(1, 2, 8)
-        f8a(0)
         load_m(5)
         load_i(6)
         load_m(6)
         load_i(7)
         load_m(7)
 
-        p1(0, 0, 7)
+        p1(0, 0, 4)
+        p1(0, 4, 8)
         f2(1)
         f3(1)
         f4(1)
         f1(2, 0, 4)
         f5(1)
-        p1(0, 7, 8)
-        p2v(0, 0, 3)
+        p2(0, [0, 1, 2, 3])
+        nmean(0, 0, 4)
         f6(1)
         f7(1)
         f8(1)
         f9(1)
         f7a(1)
         f1(2, 4, 8)
-        p2g(0, 3)
-        nmean(0, 0, 8)
         p3(0, [0, 1])
-        p2v(0, 4, 7)
-        f8a(1)
+        p2(0, [4, 5, 6, 7])
 
         LAST = NT - 1
         for i in range(1, NT - 1):
             p1(i, 0, 4)
-            p3(i - 1, [0] if i > 1 else [])
+            if i > 1:
+                nmean(i - 1, 0, 4)
+                p3(i - 1, [0])
             f2(i + 1)
             f3(i + 1)
             f4(i + 1)
             p3(i - 1, [1, 2, 3] if i > 1 else [2, 3])
+            chain(i - 1, 0, 4)
             if i + 2 < NT:
                 f1(i + 2, 0, 4)
             if i >= 2:
-                p4(nc.gpsimd, i - 2, [5, 6, 7])
-                p4s(i - 2, [4])
+                p4(nc.gpsimd, i - 2, [6, 7])
+                p4s(i - 2, [4, 5])
                 store(i - 2, 4, 8)
-            p2g(i - 1, 7)
-            chain(i - 1, 0, 4)
             f5(i + 1)
             if i == 1:
                 p1(i, 4, 8)
             else:
-                p2v(i - 1, 4, 7)
+                p2(i - 1, [4, 5, 6, 7])
+            nmean(i - 1, 4, 8)
             p3(i - 1, [4, 5])
             f6(i + 1)
             f7(i + 1)
@@ -463,7 +436,6 @@ def tile_ultralightweightmemory_pa_t_kernel(
             p4(nc.gpsimd, i - 1, [1, 2, 3])
             if i + 2 < NT:
                 f1(i + 2, 4, 8)
-            p2g(i, 3)
             p3(i - 1, [6])
             p4s(i - 1, [0])
             p3(i - 1, [7])
@@ -471,38 +443,37 @@ def tile_ultralightweightmemory_pa_t_kernel(
             store(i - 1, 0, 4)
             if i >= 2:
                 p1(i, 4, 8)
-            p2v(i, 0, 3)
-            nmean(i, 0, 8)
-            f8a(i + 1)
+            p2(i, [0, 1, 2, 3])
 
         p1(LAST, 0, 4)
+        nmean(LAST - 1, 0, 4)
         p3(LAST - 1, [0, 1, 2, 3])
-        p4(nc.gpsimd, LAST - 2, [5, 6, 7])
-        p2g(LAST - 1, 7)
+        p4(nc.gpsimd, LAST - 2, [6, 7])
+        p4s(LAST - 2, [4, 5])
+        store(LAST - 2, 4, 8)
         nc.scalar.activation(out=junk[:, 0, 0:1], in_=neghalf[:, 0:1], func=ACT.Square)
         nc.scalar.activation(out=junk[:, 1, 0:1], in_=junk[:, 0, 0:1], func=ACT.Sqrt)
-        p2v(LAST - 1, 4, 7)
+        p2(LAST - 1, [4, 5, 6, 7])
         root(LAST - 1, 0, 4)
         p4(nc.gpsimd, LAST - 1, [1, 2, 3])
-        p4s(LAST - 2, [4])
-        store(LAST - 2, 4, 8)
-        nmean(LAST, 0, 4)
-        p2v(LAST, 0, 4)
-        p3(LAST - 1, [4, 5, 6, 7])
+        nmean(LAST - 1, 4, 8)
+        p2(LAST, [0, 1, 2, 3])
+        p3(LAST - 1, [4, 5])
         p4s(LAST - 1, [0])
         store(LAST - 1, 0, 4)
-        p1(LAST, 4, 7)
+        p3(LAST - 1, [6, 7])
+        nmean(LAST, 0, 4)
+        p1(LAST, 4, 8)
         root(LAST - 1, 4, 8)
         p4(nc.gpsimd, LAST - 1, [4, 5, 6, 7])
         store(LAST - 1, 4, 8)
-        p1(LAST, 7, 8)
-        p3(LAST, [0, 1, 2])
-        nmean(LAST, 4, 8)
-        p2v(LAST, 4, 6)
-        p3(LAST, [3])
-        p2v(LAST, 6, 8)
+        p3(LAST, [0, 1, 2, 3])
+        p2(LAST, [4, 5])
+        nmean(LAST, 4, 6)
+        p2(LAST, [6, 7])
         root(LAST, 0, 4)
         p3(LAST, [4, 5])
+        nmean(LAST, 6, 8)
         p3v(LAST, [6])
         p4(nc.vector, LAST, [0, 1, 2, 3])
         store(LAST, 0, 4)

@@ -55,7 +55,7 @@ def tile_ultralightweightmemory_pa_t_kernel(
         def load_w(w):
             nc.sync.dma_start(
                 out=w_raw[w][:],
-                in_=w_dram[w].rearrange("(p c) k -> p c k" if w == 0 else "(c p) k -> p c k", p=P),
+                in_=w_dram[w].rearrange("(p c) k -> p c k", p=P),
             )
 
         def load_i(i):
@@ -121,13 +121,13 @@ def tile_ultralightweightmemory_pa_t_kernel(
                         nc.tensor.transpose(
                             wt[:, c2, u, :], words[:, base + u : base + 256 : 2], ident_f[:]
                         )
-                dst = (
-                    grouped[:]
-                    .rearrange("p r t -> p (r t)")
-                    .bitcast(F32)[:, 512 * h : 512 * (h + 1)]
-                    .rearrange("p (c r u) -> p c r u", c=2, u=2)
-                )
-                src = wt[:].rearrange("p c u r -> p c r u")
+                g_words = grouped[:].rearrange("p r t -> p (r t)").bitcast(F32)
+                if w == 0:
+                    dst = g_words.rearrange("p (c r u) -> p c r u", c=KC, u=2)[:, 2 * h : 2 * h + 2]
+                    src = wt[:].rearrange("p c u r -> p c r u")
+                else:
+                    dst = g_words.rearrange("p (r c u) -> p r c u", c=KC, u=2)[:, :, 2 * h : 2 * h + 2]
+                    src = wt[:].rearrange("p c u r -> p r c u")
                 if h == 0:
                     nc.vector.tensor_copy(out=dst, in_=src)
                 else:
@@ -266,6 +266,15 @@ def tile_ultralightweightmemory_pa_t_kernel(
                 out=st[i]["nm"][:, m0:m1], in_=st[i]["sums"][:, m0:m1], mul=-1.0 / D
             )
 
+        def nmean_v(i, m0, m1):
+            nc.vector.tensor_scalar(
+                out=st[i]["nm"][:, m0:m1],
+                in0=st[i]["sums"][:, m0:m1],
+                scalar1=-1.0 / D,
+                scalar2=None,
+                op0=ALU.mult,
+            )
+
         def p3(i, ms):
             for m in ms:
                 nc.scalar.activation(
@@ -316,8 +325,8 @@ def tile_ultralightweightmemory_pa_t_kernel(
             )
             if m0 == 0:
                 rstd = spool.tile([P, M], F32, name="rstd")
-                st[i]["rstd"] = rstd
                 nb = spool.tile([P, M], F32, name="nb")
+                st[i]["rstd"] = rstd
                 st[i]["nb"] = nb
             nc.vector.reciprocal(out=st[i]["rstd"][:, m0:m1], in_=std[:, m0:m1])
             nc.vector.tensor_tensor(
@@ -391,16 +400,17 @@ def tile_ultralightweightmemory_pa_t_kernel(
         f2(1)
         f3(1)
         f4(1)
-        f1(2, 0, 4)
+        f1(2, 0, 5)
         f5(1)
-        p2(0, [0, 1, 2, 3])
-        nmean(0, 0, 4)
+        p2(0, [0, 1, 2])
         f6(1)
+        p2(0, [3])
+        nmean(0, 0, 4)
         f7(1)
         f8(1)
         f9(1)
+        f1(2, 5, 8)
         f7a(1)
-        f1(2, 4, 8)
         p3(0, [0, 1])
         p2(0, [4, 5, 6, 7])
 
@@ -432,10 +442,10 @@ def tile_ultralightweightmemory_pa_t_kernel(
             f7(i + 1)
             f8(i + 1)
             f9(i + 1)
-            f7a(i + 1)
-            p4(nc.gpsimd, i - 1, [1, 2, 3])
             if i + 2 < NT:
                 f1(i + 2, 4, 8)
+            f7a(i + 1)
+            p4(nc.gpsimd, i - 1, [1, 2, 3])
             p3(i - 1, [6])
             p4s(i - 1, [0])
             p3(i - 1, [7])
@@ -445,42 +455,41 @@ def tile_ultralightweightmemory_pa_t_kernel(
                 p1(i, 4, 8)
             p2(i, [0, 1, 2, 3])
 
-        p1(LAST, 0, 4)
+        p2(LAST - 1, [4, 5, 6, 7])
         nmean(LAST - 1, 0, 4)
         p3(LAST - 1, [0, 1, 2, 3])
         p4(nc.gpsimd, LAST - 2, [6, 7])
+        chain(LAST - 1, 0, 4)
+        nmean(LAST - 1, 4, 8)
+        p3(LAST - 1, [4, 5, 6, 7])
+        p1(LAST, 0, 4)
         p4s(LAST - 2, [4, 5])
         store(LAST - 2, 4, 8)
         nc.scalar.activation(out=junk[:, 0, 0:1], in_=neghalf[:, 0:1], func=ACT.Square)
         nc.scalar.activation(out=junk[:, 1, 0:1], in_=junk[:, 0, 0:1], func=ACT.Sqrt)
-        p2(LAST - 1, [4, 5, 6, 7])
-        root(LAST - 1, 0, 4)
         p4(nc.gpsimd, LAST - 1, [1, 2, 3])
-        nmean(LAST - 1, 4, 8)
-        p2(LAST, [0, 1, 2, 3])
-        p3(LAST - 1, [4, 5])
         p4s(LAST - 1, [0])
         store(LAST - 1, 0, 4)
-        p3(LAST - 1, [6, 7])
-        nmean(LAST, 0, 4)
         p1(LAST, 4, 8)
+        p2(LAST, [0, 1])
         root(LAST - 1, 4, 8)
-        p4(nc.gpsimd, LAST - 1, [4, 5, 6, 7])
+        p4(nc.gpsimd, LAST - 1, [5, 6, 7])
+        p4s(LAST - 1, [4])
         store(LAST - 1, 4, 8)
-        p3(LAST, [0, 1, 2, 3])
+        p2(LAST, [2, 3])
+        nmean(LAST, 0, 4)
+        p3(LAST, [0, 1])
         p2(LAST, [4, 5])
-        nmean(LAST, 4, 6)
+        p3(LAST, [2, 3])
         p2(LAST, [6, 7])
+        nmean_v(LAST, 4, 8)
         root(LAST, 0, 4)
-        p3(LAST, [4, 5])
-        nmean(LAST, 6, 8)
-        p3v(LAST, [6])
+        p3(LAST, [4, 5, 6])
+        p3v(LAST, [7])
         p4(nc.vector, LAST, [0, 1, 2, 3])
         store(LAST, 0, 4)
-        p3(LAST, [7])
         root(LAST, 4, 8)
         p4(nc.vector, LAST, [4, 5])
         store(LAST, 4, 6)
-        p4(nc.vector, LAST, [6])
-        p4s(LAST, [7])
+        p4(nc.vector, LAST, [6, 7])
         store(LAST, 6, 8)

@@ -217,6 +217,30 @@ def tile_ultralightweightmemory_pa_t_kernel(
             )
             fr[j]["a_ps"] = a_ps
 
+        def f7d(j):
+            codes, scales = fr[j]["pq"]
+            acc = ps1.tile([P, KC, P], F32, name="et_ps")
+            nc.tensor.matmul_mx(
+                out=acc[:].rearrange("p c b -> p (c b)"),
+                lhsT=codes[:].bitcast(FP8X4),
+                lhsT_scale=scales[:],
+                rhs=w_codes[1][:].bitcast(FP8X4),
+                rhs_scale=w_scales[1][:],
+                start=True,
+                stop=True,
+            )
+            fr[j]["et_ps"] = acc
+
+        def f8d(j):
+            g_sb = const.tile([P, D], F32, name="g_sb")
+            nc.scalar.activation(
+                out=g_sb[:],
+                in_=fr[j]["et_ps"][:].rearrange("p c b -> p (c b)"),
+                func=ACT.Sigmoid,
+                scale=-1.0,
+            )
+            fr[j]["g_ps"] = g_sb
+
         def f8(j):
             g_t = fpool.tile([P, KC, P], F32, name="g_t")
             nc.scalar.activation(out=g_t[:], in_=fr[j]["et_ps"][:], func=ACT.Sigmoid, scale=-1.0)
@@ -260,6 +284,20 @@ def tile_ultralightweightmemory_pa_t_kernel(
                     op1=ALU.add,
                     accum_out=st[i]["sums"][:, m : m + 1],
                 )
+
+        def p2w(i, m):
+            x = st[i]["x"]
+            nc.vector.tensor_tensor(
+                out=x[:, m, :], in0=x[:, m, :], in1=fr[i]["a_ps"][:], op=ALU.add
+            )
+
+        def sum_s(i, m):
+            nc.scalar.activation(
+                out=junk[:, m % 2, :],
+                in_=st[i]["x"][:, m, :],
+                func=ACT.Identity,
+                accum_out=st[i]["sums"][:, m : m + 1],
+            )
 
         def nmean(i, m0, m1):
             nc.scalar.mul(
@@ -383,10 +421,9 @@ def tile_ultralightweightmemory_pa_t_kernel(
         f5(0)
         f6(0)
         prep_weight(2)
-        f7(0)
+        f7d(0)
         f1(1, 0, 2)
-        f8(0)
-        f9(0)
+        f8d(0)
         f7a(0)
         f1(1, 2, 8)
         load_m(5)
@@ -455,41 +492,45 @@ def tile_ultralightweightmemory_pa_t_kernel(
                 p1(i, 4, 8)
             p2(i, [0, 1, 2, 3])
 
-        p2(LAST - 1, [4, 5, 6, 7])
+        nc.scalar.activation(out=junk[:, 0, 0:1], in_=neghalf[:, 0:1], func=ACT.Square)
+        nc.scalar.activation(out=junk[:, 1, 0:1], in_=junk[:, 0, 0:1], func=ACT.Sqrt)
         nmean(LAST - 1, 0, 4)
         p3(LAST - 1, [0, 1, 2, 3])
+        p2(LAST - 1, [4, 5, 6, 7])
         p4(nc.gpsimd, LAST - 2, [6, 7])
-        chain(LAST - 1, 0, 4)
+        root(LAST - 1, 0, 4)
+        p4s(LAST - 2, [4, 5])
+        store(LAST - 2, 4, 8)
         nmean(LAST - 1, 4, 8)
         p3(LAST - 1, [4, 5, 6, 7])
         p1(LAST, 0, 4)
-        p4s(LAST - 2, [4, 5])
-        store(LAST - 2, 4, 8)
-        nc.scalar.activation(out=junk[:, 0, 0:1], in_=neghalf[:, 0:1], func=ACT.Square)
-        nc.scalar.activation(out=junk[:, 1, 0:1], in_=junk[:, 0, 0:1], func=ACT.Sqrt)
         p4(nc.gpsimd, LAST - 1, [1, 2, 3])
         p4s(LAST - 1, [0])
         store(LAST - 1, 0, 4)
         p1(LAST, 4, 8)
-        p2(LAST, [0, 1])
         root(LAST - 1, 4, 8)
+        p2(LAST, [0, 1])
         p4(nc.gpsimd, LAST - 1, [5, 6, 7])
         p4s(LAST - 1, [4])
         store(LAST - 1, 4, 8)
-        p2(LAST, [2, 3])
-        nmean(LAST, 0, 4)
+        nmean(LAST, 0, 2)
         p3(LAST, [0, 1])
-        p2(LAST, [4, 5])
+        p2(LAST, [2, 3])
+        nmean(LAST, 2, 4)
         p3(LAST, [2, 3])
-        p2(LAST, [6, 7])
-        nmean_v(LAST, 4, 8)
+        p2(LAST, [4, 5])
+        nmean(LAST, 4, 6)
+        p2(LAST, [6])
         root(LAST, 0, 4)
-        p3(LAST, [4, 5, 6])
-        p3v(LAST, [7])
+        p2(LAST, [7])
+        p3(LAST, [4, 5])
+        nmean(LAST, 6, 8)
         p4(nc.vector, LAST, [0, 1, 2, 3])
         store(LAST, 0, 4)
+        p3(LAST, [6, 7])
         root(LAST, 4, 8)
         p4(nc.vector, LAST, [4, 5])
         store(LAST, 4, 6)
-        p4(nc.vector, LAST, [6, 7])
+        p4(nc.vector, LAST, [6])
+        p4s(LAST, [7])
         store(LAST, 6, 8)

@@ -66,17 +66,21 @@ def tile_ultralightweightmemory_pa_t_kernel(
                 )
             i_tiles.append(it)
 
-        def load_m(i):
+        def load_m(i, parts=1):
             mt = mpool.tile([P, M, D], BF16, name="mt")
-            nc.sync.dma_start(out=mt[:], in_=mview[i])
+            n = M // parts
+            for h in range(parts):
+                nc.sync.dma_start(
+                    out=mt[:, n * h : n * (h + 1), :], in_=mview[i][:, n * h : n * (h + 1), :]
+                )
             m_tiles.append(mt)
 
         load_w(0)
         load_i(0)
         load_w(1)
+        load_m(0, 2)
         load_w(2)
         load_i(1)
-        load_m(0)
         load_i(2)
         load_m(1)
         for i in range(3, 6):
@@ -110,7 +114,7 @@ def tile_ultralightweightmemory_pa_t_kernel(
             w_codes.append(wc)
             w_scales.append(ws)
 
-        def prep_weight(w):
+        def prep_copy(w, engines):
             grouped = wpool.tile([P, 512, KC], BF16, name="grouped", align_bytes=64)
             words = w_raw[w][:].rearrange("p c k -> p (c k)").bitcast(F32)
             for h in range(2):
@@ -128,10 +132,13 @@ def tile_ultralightweightmemory_pa_t_kernel(
                 else:
                     dst = g_words.rearrange("p (r c u) -> p r c u", c=KC, u=2)[:, :, 2 * h : 2 * h + 2]
                     src = wt[:].rearrange("p c u r -> p r c u")
-                if h == 0:
+                if engines[h] == 0:
                     nc.vector.tensor_copy(out=dst, in_=src)
                 else:
                     nc.scalar.copy(out=dst, in_=src)
+            return grouped
+
+        def prep_quant(w, grouped):
             nc.vector.quantize_mx(
                 out=w_codes[w][:].bitcast(FP8X4),
                 scales=w_scales[w][:],
@@ -412,19 +419,18 @@ def tile_ultralightweightmemory_pa_t_kernel(
         def store(i, m0, m1):
             nc.sync.dma_start(out=oview[i][:, m0:m1, :], in_=st[i]["x"][:, m0:m1, :])
 
-        prep_weight(0)
+        prep_quant(0, prep_copy(0, [0, 1]))
         f1(0, 0, 8)
         f2(0)
         f3(0)
-        prep_weight(1)
+        prep_quant(1, prep_copy(1, [0, 0]))
         f4(0)
         f5(0)
         f6(0)
-        prep_weight(2)
         f7d(0)
         f1(1, 0, 2)
         f8d(0)
-        f7a(0)
+        grouped2 = prep_copy(2, [1, 1])
         f1(1, 2, 8)
         load_m(5)
         load_i(6)
@@ -433,6 +439,8 @@ def tile_ultralightweightmemory_pa_t_kernel(
         load_m(7)
 
         p1(0, 0, 4)
+        prep_quant(2, grouped2)
+        f7a(0)
         p1(0, 4, 8)
         f2(1)
         f3(1)
@@ -457,18 +465,19 @@ def tile_ultralightweightmemory_pa_t_kernel(
             if i > 1:
                 nmean(i - 1, 0, 4)
                 p3(i - 1, [0])
-            f2(i + 1)
+            if i == 1:
+                f2(i + 1)
             f3(i + 1)
             f4(i + 1)
             p3(i - 1, [1, 2, 3] if i > 1 else [2, 3])
+            f5(i + 1)
             chain(i - 1, 0, 4)
             if i + 2 < NT:
-                f1(i + 2, 0, 4)
+                f1(i + 2, 0, 6)
             if i >= 2:
                 p4(nc.gpsimd, i - 2, [6, 7])
                 p4s(i - 2, [4, 5])
                 store(i - 2, 4, 8)
-            f5(i + 1)
             if i == 1:
                 p1(i, 4, 8)
             else:
@@ -480,7 +489,7 @@ def tile_ultralightweightmemory_pa_t_kernel(
             f8(i + 1)
             f9(i + 1)
             if i + 2 < NT:
-                f1(i + 2, 4, 8)
+                f1(i + 2, 6, 8)
             f7a(i + 1)
             p4(nc.gpsimd, i - 1, [1, 2, 3])
             p3(i - 1, [6])
@@ -491,6 +500,8 @@ def tile_ultralightweightmemory_pa_t_kernel(
             if i >= 2:
                 p1(i, 4, 8)
             p2(i, [0, 1, 2, 3])
+            if i + 2 < NT:
+                f2(i + 2)
 
         nc.scalar.activation(out=junk[:, 0, 0:1], in_=neghalf[:, 0:1], func=ACT.Square)
         nc.scalar.activation(out=junk[:, 1, 0:1], in_=junk[:, 0, 0:1], func=ACT.Sqrt)
@@ -498,18 +509,19 @@ def tile_ultralightweightmemory_pa_t_kernel(
         p3(LAST - 1, [0, 1, 2, 3])
         p2(LAST - 1, [4, 5, 6, 7])
         p4(nc.gpsimd, LAST - 2, [6, 7])
+        p1(LAST, 0, 4)
         root(LAST - 1, 0, 4)
         p4s(LAST - 2, [4, 5])
         store(LAST - 2, 4, 8)
         nmean(LAST - 1, 4, 8)
         p3(LAST - 1, [4, 5, 6, 7])
-        p1(LAST, 0, 4)
         p4(nc.gpsimd, LAST - 1, [1, 2, 3])
         p4s(LAST - 1, [0])
         store(LAST - 1, 0, 4)
         p1(LAST, 4, 8)
+        p2(LAST, [0])
         root(LAST - 1, 4, 8)
-        p2(LAST, [0, 1])
+        p2(LAST, [1])
         p4(nc.gpsimd, LAST - 1, [5, 6, 7])
         p4s(LAST - 1, [4])
         store(LAST - 1, 4, 8)
@@ -520,13 +532,14 @@ def tile_ultralightweightmemory_pa_t_kernel(
         p3(LAST, [2, 3])
         p2(LAST, [4, 5])
         nmean(LAST, 4, 6)
-        p2(LAST, [6])
+        p2(LAST, [6, 7])
         root(LAST, 0, 4)
-        p2(LAST, [7])
         p3(LAST, [4, 5])
         nmean(LAST, 6, 8)
-        p4(nc.vector, LAST, [0, 1, 2, 3])
-        store(LAST, 0, 4)
+        p4(nc.vector, LAST, [0, 1])
+        store(LAST, 0, 2)
+        p4(nc.vector, LAST, [2, 3])
+        store(LAST, 2, 4)
         p3(LAST, [6, 7])
         root(LAST, 4, 8)
         p4(nc.vector, LAST, [4, 5])

@@ -66,21 +66,19 @@ def tile_ultralightweightmemory_pa_t_kernel(
                 )
             i_tiles.append(it)
 
-        def load_m(i, parts=1):
-            mt = mpool.tile([P, M, D], BF16, name="mt")
-            n = M // parts
-            for h in range(parts):
-                nc.sync.dma_start(
-                    out=mt[:, n * h : n * (h + 1), :], in_=mview[i][:, n * h : n * (h + 1), :]
-                )
-            m_tiles.append(mt)
+        def load_m(i, m0=0, m1=M):
+            if m0 == 0:
+                mt = mpool.tile([P, M, D], BF16, name="mt")
+                m_tiles.append(mt)
+            nc.sync.dma_start(out=m_tiles[i][:, m0:m1, :], in_=mview[i][:, m0:m1, :])
 
         load_w(0)
         load_i(0)
         load_w(1)
-        load_m(0, 2)
-        load_w(2)
+        load_m(0, 0, 4)
         load_i(1)
+        load_w(2)
+        load_m(0, 4, 8)
         load_i(2)
         load_m(1)
         for i in range(3, 6):
@@ -441,27 +439,31 @@ def tile_ultralightweightmemory_pa_t_kernel(
         p1(0, 0, 4)
         prep_quant(2, grouped2)
         f7a(0)
-        p1(0, 4, 8)
+        p1(0, 4, 6)
         f2(1)
         f3(1)
         f4(1)
-        f1(2, 0, 5)
+        p1(0, 6, 8)
+        f1(2, 0, 6)
         f5(1)
-        p2(0, [0, 1, 2])
+        p2(0, [0, 1])
         f6(1)
-        p2(0, [3])
+        p2(0, [2, 3])
         nmean(0, 0, 4)
         f7(1)
         f8(1)
         f9(1)
-        f1(2, 5, 8)
+        f1(2, 6, 8)
         f7a(1)
         p3(0, [0, 1])
         p2(0, [4, 5, 6, 7])
 
         LAST = NT - 1
         for i in range(1, NT - 1):
-            p1(i, 0, 4)
+            if i == 1:
+                p1(i, 0, 2)
+            else:
+                p1(i, 0, 4)
             if i > 1:
                 nmean(i - 1, 0, 4)
                 p3(i - 1, [0])
@@ -469,6 +471,8 @@ def tile_ultralightweightmemory_pa_t_kernel(
                 f2(i + 1)
             f3(i + 1)
             f4(i + 1)
+            if i == 1:
+                p1(i, 2, 4)
             p3(i - 1, [1, 2, 3] if i > 1 else [2, 3])
             f5(i + 1)
             chain(i - 1, 0, 4)
@@ -479,12 +483,14 @@ def tile_ultralightweightmemory_pa_t_kernel(
                 p4s(i - 2, [4, 5])
                 store(i - 2, 4, 8)
             if i == 1:
-                p1(i, 4, 8)
+                p1(i, 4, 6)
             else:
                 p2(i - 1, [4, 5, 6, 7])
             nmean(i - 1, 4, 8)
             p3(i - 1, [4, 5])
             f6(i + 1)
+            if i == 1:
+                p1(i, 6, 8)
             f7(i + 1)
             f8(i + 1)
             f9(i + 1)
@@ -514,11 +520,12 @@ def tile_ultralightweightmemory_pa_t_kernel(
         p4s(LAST - 2, [4, 5])
         store(LAST - 2, 4, 8)
         nmean(LAST - 1, 4, 8)
-        p3(LAST - 1, [4, 5, 6, 7])
+        p3(LAST - 1, [4, 5, 6])
         p4(nc.gpsimd, LAST - 1, [1, 2, 3])
         p4s(LAST - 1, [0])
         store(LAST - 1, 0, 4)
         p1(LAST, 4, 8)
+        p3v(LAST - 1, [7])
         p2(LAST, [0])
         root(LAST - 1, 4, 8)
         p2(LAST, [1])
@@ -540,7 +547,8 @@ def tile_ultralightweightmemory_pa_t_kernel(
         store(LAST, 0, 2)
         p4(nc.vector, LAST, [2, 3])
         store(LAST, 2, 4)
-        p3(LAST, [6, 7])
+        p3(LAST, [6])
+        p3v(LAST, [7])
         root(LAST, 4, 8)
         p4(nc.vector, LAST, [4, 5])
         store(LAST, 4, 6)

from contextlib import ExitStack

import concourse.mybir as mybir
from concourse.masks import make_identity

F32 = mybir.dt.float32
BF16 = mybir.dt.bfloat16
U32 = mybir.dt.uint32
U8 = mybir.dt.uint8
FP8X4 = mybir.dt.float8_e4m3fn_x4
ALU = mybir.AluOpType
ACT = mybir.ActivationFunctionType
AX = mybir.AxisListType

B, S, D, M, R = 1024, 8, 512, 8, 512
LN_EPS = 1e-5
P = 128
NT = B // P
KC = 4
GB = P // S
NG = P // GB
FLOPS = 3 * 2 * B * D * R


def tile_ultralightweightmemory_pa_t_kernel(
    tc, interface, memory, W_write_key, W_write_erase, W_write_add, out
):
    nc = tc.nc
    iview = interface.rearrange("b s d -> (b s) d").rearrange(
        "(n g p) d -> n p g d", n=NT, g=NG, p=P
    )
    mview = memory.rearrange("(n p) m d -> n p m d", p=P)
    oview = out.rearrange("(n p) m d -> n p m d", p=P)

    with ExitStack() as ctx:
        const = ctx.enter_context(tc.tile_pool(name="const", bufs=1))
        ipool = ctx.enter_context(tc.tile_pool(name="ipool", bufs=6))
        mpool = ctx.enter_context(tc.tile_pool(name="mpool", bufs=NT))
        xpool = ctx.enter_context(tc.tile_pool(name="xpool", bufs=5))
        wpool = ctx.enter_context(tc.tile_pool(name="wpool", bufs=2))
        fpool = ctx.enter_context(tc.tile_pool(name="fpool", bufs=2))
        spool = ctx.enter_context(tc.tile_pool(name="spool", bufs=4))
        ps1 = ctx.enter_context(tc.psum_pool(name="ps1", bufs=1))
        ps2 = ctx.enter_context(tc.psum_pool(name="ps2", bufs=2))
        ctx.enter_context(tc.manual_schedule())

        w_dram = [W_write_key, W_write_erase, W_write_add]
        w_raw = []
        for w in range(3):
            wr = const.tile([P, KC, 512], BF16, name="w_raw%d" % w)
            w_raw.append(wr)
        i_tiles = []
        m_tiles = []

        def load_w(w):
            nc.sync.dma_start(
                out=w_raw[w][:],
                in_=w_dram[w].rearrange("(p c) k -> p c k", p=P),
            )

        def load_i(i):
            it = ipool.tile([P, NG, D], BF16, name="it")
            for h in range(2):
                nc.sync.dma_start(
                    out=it[:, 4 * h : 4 * h + 4, :], in_=iview[i][:, 4 * h : 4 * h + 4, :]
                )
            i_tiles.append(it)

        def load_m(i, m0=0, m1=M):
            if m0 == 0:
                mt = mpool.tile([P, M, D], BF16, name="mt")
                m_tiles.append(mt)
            nc.sync.dma_start(out=m_tiles[i][:, m0:m1, :], in_=mview[i][:, m0:m1, :])

        load_w(0)
        load_i(0)
        load_w(1)
        load_m(0, 0, 4)
        load_i(1)
        load_w(2)
        load_m(0, 4, 8)
        load_i(2)
        load_m(1)
        for i in range(3, 6):
            load_i(i)
            load_m(i - 1)

        junk = const.tile([P, 2, D], BF16, name="junk")
        junk_v = const.tile([P, D], BF16, name="junk_v")
        neghalf = const.tile([P, M], F32, name="neghalf")
        nc.vector.memset(neghalf[:], -0.5)
        nc.scalar.activation(out=junk[:, 0, 0:1], in_=neghalf[:, 0:1], func=ACT.Sigmoid)
        ident_f = const.tile([P, P], F32, name="ident_f")
        make_identity(nc, ident_f[:])
        avg_f = const.tile([P, GB], F32, name="avg_f")
        nc.vector.tensor_reduce(
            out=avg_f[:],
            in_=ident_f[:].rearrange("p (j s) -> p j s", s=S),
            axis=AX.X,
            op=ALU.add,
        )
        avg = const.tile([P, GB], BF16, name="avg")
        nc.vector.tensor_scalar(
            out=avg[:], in0=avg_f[:], scalar1=1.0 / S, scalar2=None, op0=ALU.mult
        )

        w_codes = []
        w_scales = []
        for w in range(3):
            wc = const.tile([P, 512], U32, name="w_codes%d" % w, align_bytes=64)
            ws = const.tile([P, 512], U8, name="w_scales%d" % w, align_bytes=64)
            w_codes.append(wc)
            w_scales.append(ws)

        def prep_copy(w, engines):
            grouped = wpool.tile([P, 512, KC], BF16, name="grouped", align_bytes=64)
            words = w_raw[w][:].rearrange("p c k -> p (c k)").bitcast(F32)
            for h in range(2):
                wt = ps2.tile([P, 2, 2, P], F32, name="wt", tag=("g_ps" if h == 0 else "a_ps"))
                for c2 in range(2):
                    for u in range(2):
                        base = (2 * h + c2) * 256
                        nc.tensor.transpose(
                            wt[:, c2, u, :], words[:, base + u : base + 256 : 2], ident_f[:]
                        )
                g_words = grouped[:].rearrange("p r t -> p (r t)").bitcast(F32)
                if w == 0:
                    dst = g_words.rearrange("p (c r u) -> p c r u", c=KC, u=2)[:, 2 * h : 2 * h + 2]
                    src = wt[:].rearrange("p c u r -> p c r u")
                else:
                    dst = g_words.rearrange("p (r c u) -> p r c u", c=KC, u=2)[:, :, 2 * h : 2 * h + 2]
                    src = wt[:].rearrange("p c u r -> p r c u")
                if engines[h] == 0:
                    nc.vector.tensor_copy(out=dst, in_=src)
                else:
                    nc.scalar.copy(out=dst, in_=src)
            return grouped

        def prep_quant(w, grouped):
            nc.vector.quantize_mx(
                out=w_codes[w][:].bitcast(FP8X4),
                scales=w_scales[w][:],
                in_=grouped[:].rearrange("p r t -> p (r t)"),
            )

        fr = {}

        def f1(j, g0, g1):
            it = i_tiles[j]
            if g0 == 0:
                mean_ps = ps1.tile([P, KC, P], F32, name="mean_ps")
                fr[j] = {"mean_ps": mean_ps}
            mean_ps = fr[j]["mean_ps"]
            for g in range(g0, g1):
                for t in range(KC):
                    nc.tensor.matmul(
                        out=mean_ps[:, t, GB * g : GB * (g + 1)],
                        lhsT=it[:, g, t : D : KC],
                        rhs=avg[:],
                        start=True,
                        stop=True,
                    )

        def f2(j):
            im_g = fpool.tile([P, P, KC], BF16, name="im_g", align_bytes=64)
            nc.scalar.copy(out=im_g[:], in_=fr[j]["mean_ps"][:].rearrange("p t b -> p b t"))
            fr[j]["im_g"] = im_g

        def quant(j, src, dst):
            codes = fpool.tile([P, P], U32, name=dst + "_c", align_bytes=64)
            scales = fpool.tile([P, P], U8, name=dst + "_s", align_bytes=64)
            nc.vector.quantize_mx(
                out=codes[:].bitcast(FP8X4),
                scales=scales[:],
                in_=fr[j][src][:].rearrange("p b t -> p (b t)"),
            )
            fr[j][dst] = (codes, scales)

        def mx_t(j, w, src, dst):
            codes, scales = fr[j][src]
            acc = ps1.tile([P, KC, P], F32, name=dst)
            for c in range(KC):
                nc.tensor.matmul_mx(
                    out=acc[:, c, :],
                    lhsT=w_codes[w][:, c * P : (c + 1) * P].bitcast(FP8X4),
                    lhsT_scale=w_scales[w][:, c * P : (c + 1) * P],
                    rhs=codes[:].bitcast(FP8X4),
                    rhs_scale=scales[:],
                    start=True,
                    stop=True,
                )
            fr[j][dst] = acc

        def f3(j):
            quant(j, "im_g", "im")

        def f4(j):
            mx_t(j, 0, "im", "s1_ps")

        def f5(j):
            pj_g = fpool.tile([P, P, KC], BF16, name="pj_g", align_bytes=64)
            nc.scalar.copy(out=pj_g[:], in_=fr[j]["s1_ps"][:].rearrange("p c b -> p b c"))
            fr[j]["pj_g"] = pj_g

        def f6(j):
            quant(j, "pj_g", "pq")

        def f7(j):
            mx_t(j, 1, "pq", "et_ps")

        def f7a(j):
            codes, scales = fr[j]["pq"]
            a_ps = ps2.tile([P, D], F32, name="a_ps")
            nc.tensor.matmul_mx(
                out=a_ps[:],
                lhsT=codes[:].bitcast(FP8X4),
                lhsT_scale=scales[:],
                rhs=w_codes[2][:].bitcast(FP8X4),
                rhs_scale=w_scales[2][:],
                start=True,
                stop=True,
            )
            fr[j]["a_ps"] = a_ps

        def f7d(j):
            codes, scales = fr[j]["pq"]
            acc = ps1.tile([P, KC, P], F32, name="et_ps")
            nc.tensor.matmul_mx(
                out=acc[:].rearrange("p c b -> p (c b)"),
                lhsT=codes[:].bitcast(FP8X4),
                lhsT_scale=scales[:],
                rhs=w_codes[1][:].bitcast(FP8X4),
                rhs_scale=w_scales[1][:],
                start=True,
                stop=True,
            )
            fr[j]["et_ps"] = acc

        def f8d(j):
            g_sb = const.tile([P, D], F32, name="g_sb")
            nc.scalar.activation(
                out=g_sb[:],
                in_=fr[j]["et_ps"][:].rearrange("p c b -> p (c b)"),
                func=ACT.Sigmoid,
                scale=-1.0,
            )
            fr[j]["g_ps"] = g_sb

        def f8(j):
            g_t = fpool.tile([P, KC, P], F32, name="g_t")
            nc.scalar.activation(out=g_t[:], in_=fr[j]["et_ps"][:], func=ACT.Sigmoid, scale=-1.0)
            fr[j]["g_t"] = g_t

        def f9(j):
            g_ps = ps2.tile([P, D], F32, name="g_ps")
            for c in range(KC):
                nc.tensor.transpose(
                    g_ps[:, c * P : (c + 1) * P], fr[j]["g_t"][:, c, :], ident_f[:]
                )
            fr[j]["g_ps"] = g_ps

        st = []
        for i in range(NT):
            st.append({})

        def p1(i, m0, m1):
            if m0 == 0:
                x = xpool.tile([P, M, D], F32, name="x")
                sums = spool.tile([P, M], F32, name="sums")
                nm = spool.tile([P, M], F32, name="nm")
                ssq = spool.tile([P, M], F32, name="ssq")
                st[i] = {"x": x, "sums": sums, "nm": nm, "ssq": ssq}
            nc.vector.tensor_tensor(
                out=st[i]["x"][:, m0:m1, :],
                in0=m_tiles[i][:, m0:m1, :],
                in1=fr[i]["g_ps"][:].unsqueeze(1).to_broadcast([P, m1 - m0, D]),
                op=ALU.mult,
            )

        def p2(i, ms):
            x = st[i]["x"]
            for m in ms:
                nc.vector.scalar_tensor_tensor(
                    out=x[:, m, :],
                    in0=x[:, m, :],
                    scalar=1.0,
                    in1=fr[i]["a_ps"][:],
                    op0=ALU.mult,
                    op1=ALU.add,
                    accum_out=st[i]["sums"][:, m : m + 1],
                )

        def p2w(i, m):
            x = st[i]["x"]
            nc.vector.tensor_tensor(
                out=x[:, m, :], in0=x[:, m, :], in1=fr[i]["a_ps"][:], op=ALU.add
            )

        def sum_s(i, m):
            nc.scalar.activation(
                out=junk[:, m % 2, :],
                in_=st[i]["x"][:, m, :],
                func=ACT.Identity,
                accum_out=st[i]["sums"][:, m : m + 1],
            )

        def nmean(i, m0, m1):
            nc.scalar.mul(
                out=st[i]["nm"][:, m0:m1], in_=st[i]["sums"][:, m0:m1], mul=-1.0 / D
            )

        def nmean_v(i, m0, m1):
            nc.vector.tensor_scalar(
                out=st[i]["nm"][:, m0:m1],
                in0=st[i]["sums"][:, m0:m1],
                scalar1=-1.0 / D,
                scalar2=None,
                op0=ALU.mult,
            )

        def p3(i, ms):
            for m in ms:
                nc.scalar.activation(
                    out=junk[:, m % 2, :],
                    in_=st[i]["x"][:, m, :],
                    func=ACT.Square,
                    bias=st[i]["nm"][:, m : m + 1],
                    scale=1.0,
                    accum_out=st[i]["ssq"][:, m : m + 1],
                )

        def chain(i, m0, m1):
            if m0 == 0:
                ve = spool.tile([P, M], F32, name="ve")
                rstd = spool.tile([P, M], F32, name="rstd")
                nb = spool.tile([P, M], F32, name="nb")
                st[i]["ve"] = ve
                st[i]["rstd"] = rstd
                st[i]["nb"] = nb
            ve = st[i]["ve"]
            rstd = st[i]["rstd"]
            nc.gpsimd.tensor_scalar(
                out=ve[:, m0:m1],
                in0=st[i]["ssq"][:, m0:m1],
                scalar1=1.0 / D,
                scalar2=LN_EPS,
                op0=ALU.mult,
                op1=ALU.add,
            )
            nc.gpsimd.tensor_tensor(
                out=rstd[:, m0:m1], in0=ve[:, m0:m1], in1=neghalf[:, m0:m1], op=ALU.pow
            )
            nc.gpsimd.tensor_tensor(
                out=st[i]["nb"][:, m0:m1],
                in0=st[i]["nm"][:, m0:m1],
                in1=rstd[:, m0:m1],
                op=ALU.mult,
            )

        def root(i, m0, m1):
            std = spool.tile([P, M], F32, name="std")
            nc.scalar.activation(
                out=std[:, m0:m1],
                in_=st[i]["ssq"][:, m0:m1],
                func=ACT.Sqrt,
                scale=1.0 / D,
                bias=LN_EPS,
            )
            if m0 == 0:
                rstd = spool.tile([P, M], F32, name="rstd")
                nb = spool.tile([P, M], F32, name="nb")
                st[i]["rstd"] = rstd
                st[i]["nb"] = nb
            nc.vector.reciprocal(out=st[i]["rstd"][:, m0:m1], in_=std[:, m0:m1])
            nc.vector.tensor_tensor(
                out=st[i]["nb"][:, m0:m1],
                in0=st[i]["nm"][:, m0:m1],
                in1=st[i]["rstd"][:, m0:m1],
                op=ALU.mult,
            )

        def p3v(i, ms):
            for m in ms:
                nc.vector.scalar_tensor_tensor(
                    out=junk_v[:],
                    in0=st[i]["x"][:, m, :],
                    scalar=st[i]["nm"][:, m : m + 1],
                    in1=st[i]["x"][:, m, :],
                    op0=ALU.add,
                    op1=ALU.mult,
                    accum_out=st[i]["ssq"][:, m : m + 1],
                )

        def p4s(i, ms):
            x = st[i]["x"]
            for m in ms:
                nc.scalar.activation(
                    out=x[:, m, :],
                    in_=x[:, m, :],
                    func=ACT.Identity,
                    bias=st[i]["nb"][:, m : m + 1],
                    scale=st[i]["rstd"][:, m : m + 1],
                )

        def p4(engine, i, ms):
            x = st[i]["x"]
            for m in ms:
                engine.tensor_scalar(
                    out=x[:, m, :],
                    in0=x[:, m, :],
                    scalar1=st[i]["nm"][:, m : m + 1],
                    scalar2=st[i]["rstd"][:, m : m + 1],
                    op0=ALU.add,
                    op1=ALU.mult,
                )

        def store(i, m0, m1):
            nc.sync.dma_start(out=oview[i][:, m0:m1, :], in_=st[i]["x"][:, m0:m1, :])

        prep_quant(0, prep_copy(0, [0, 1]))
        f1(0, 0, 8)
        f2(0)
        f3(0)
        prep_quant(1, prep_copy(1, [0, 0]))
        f4(0)
        f5(0)
        f6(0)
        f7d(0)
        f1(1, 0, 2)
        f8d(0)
        grouped2 = prep_copy(2, [1, 1])
        f1(1, 2, 8)
        load_m(5)
        load_i(6)
        load_m(6)
        load_i(7)
        load_m(7)

        p1(0, 0, 4)
        prep_quant(2, grouped2)
        f7a(0)
        p1(0, 4, 6)
        f2(1)
        f3(1)
        f4(1)
        p1(0, 6, 8)
        f1(2, 0, 6)
        f5(1)
        p2(0, [0, 1])
        f6(1)
        p2(0, [2, 3])
        nmean(0, 0, 4)
        f7(1)
        f8(1)
        f9(1)
        f1(2, 6, 8)
        f7a(1)
        p3(0, [0, 1])
        p2(0, [4, 5, 6, 7])

        LAST = NT - 1
        for i in range(1, NT - 1):
            if i == 1:
                p1(i, 0, 2)
            else:
                p1(i, 0, 4)
            if i > 1:
                nmean(i - 1, 0, 4)
                p3(i - 1, [0])
            if i == 1:
                f2(i + 1)
            f3(i + 1)
            f4(i + 1)
            if i == 1:
                p1(i, 2, 4)
            p3(i - 1, [1, 2, 3] if i > 1 else [2, 3])
            f5(i + 1)
            chain(i - 1, 0, 4)
            if i + 2 < NT:
                f1(i + 2, 0, 6)
            if i >= 2:
                p4(nc.gpsimd, i - 2, [6, 7])
                p4s(i - 2, [4, 5])
                store(i - 2, 4, 8)
            if i == 1:
                p1(i, 4, 6)
            else:
                p2(i - 1, [4, 5, 6, 7])
            nmean(i - 1, 4, 8)
            p3(i - 1, [4, 5])
            f6(i + 1)
            if i == 1:
                p1(i, 6, 8)
            f7(i + 1)
            f8(i + 1)
            f9(i + 1)
            if i + 2 < NT:
                f1(i + 2, 6, 8)
            f7a(i + 1)
            p4(nc.gpsimd, i - 1, [1, 2, 3])
            p3(i - 1, [6])
            p4s(i - 1, [0])
            p3(i - 1, [7])
            chain(i - 1, 4, 8)
            store(i - 1, 0, 4)
            if i >= 2:
                p1(i, 4, 8)
            p2(i, [0, 1, 2, 3])
            if i + 2 < NT:
                f2(i + 2)

        nc.scalar.activation(out=junk[:, 0, 0:1], in_=neghalf[:, 0:1], func=ACT.Square)
        nc.scalar.activation(out=junk[:, 1, 0:1], in_=junk[:, 0, 0:1], func=ACT.Sqrt)
        nmean(LAST - 1, 0, 4)
        p3(LAST - 1, [0, 1, 2, 3])
        p2(LAST - 1, [4, 5, 6, 7])
        p4(nc.gpsimd, LAST - 2, [6, 7])
        p1(LAST, 0, 4)
        root(LAST - 1, 0, 4)
        p4s(LAST - 2, [4, 5])
        store(LAST - 2, 4, 8)
        nmean(LAST - 1, 4, 8)
        p3(LAST - 1, [4, 5, 6])
        p4(nc.gpsimd, LAST - 1, [1, 2, 3])
        p4s(LAST - 1, [0])
        store(LAST - 1, 0, 4)
        p1(LAST, 4, 8)
        p3v(LAST - 1, [7])
        p2(LAST, [0])
        root(LAST - 1, 4, 8)
        p2(LAST, [1])
        p4(nc.gpsimd, LAST - 1, [5, 6, 7])
        p4s(LAST - 1, [4])
        store(LAST - 1, 4, 8)
        nmean(LAST, 0, 2)
        p3(LAST, [0, 1])
        p2(LAST, [2, 3])
        nmean(LAST, 2, 4)
        p3(LAST, [2, 3])
        p2(LAST, [4, 5])
        nmean(LAST, 4, 6)
        p2(LAST, [6, 7])
        root(LAST, 0, 4)
        p3(LAST, [4, 5])
        nmean(LAST, 6, 8)
        p4(nc.vector, LAST, [0, 1])
        store(LAST, 0, 2)
        p4(nc.vector, LAST, [2, 3])
        store(LAST, 2, 4)
        p3(LAST, [6])
        p3v(LAST, [7])
        root(LAST, 4, 8)
        p4(nc.vector, LAST, [4, 5])
        store(LAST, 4, 6)
        p4(nc.vector, LAST, [6])
        p4s(LAST, [7])
        store(LAST, 6, 8)
